import numpy as np
import ml_dtypes


def mxq(x, axis, fmt="e4m3"):
    dtype, down = {"e4m3": (ml_dtypes.float8_e4m3fn, 7), "e5m2": (ml_dtypes.float8_e5m2, 14)}[fmt]
    v = np.moveaxis(np.asarray(x, np.float32).astype(ml_dtypes.bfloat16).astype(np.float64), axis, -1)
    blocks = v.reshape(v.shape[:-1] + (-1, 32))
    amax = np.abs(blocks).max(-1, keepdims=True)
    byte = np.maximum(np.where(amax > 0, np.frexp(amax)[1] - 1 + 127, 0) - down, 1)
    scale = np.exp2(byte - 127.0)
    codes = (blocks / scale).astype(np.float32).astype(dtype).astype(np.float64)
    return np.moveaxis((codes * scale).reshape(v.shape), -1, axis)


WIDE = False


def mx_kscale(k):
    if not WIDE:
        return np.ones(k)
    levels = np.array([10, -10, 5, -5, 0])
    if k % 512:
        return np.exp2(np.random.permutation(np.resize(levels, k // 32))).repeat(32)
    a = np.empty((k // 512, 16))
    for p in range(k // 512):
        a[p, :8] = np.random.permutation(np.resize(levels, 8))
        for g in range(8):
            far = levels[np.abs(levels - a[p, g]) >= 10]
            a[p, g + 8] = far[np.random.randint(len(far))]
    return np.exp2(a.ravel()).repeat(32)


BF16 = ml_dtypes.bfloat16


def bf(x):
    return np.asarray(x, np.float32).astype(BF16)


def f64(x):
    return np.asarray(x).astype(np.float64)


B, S, D, H, HD, M, G = 4, 2048, 512, 1, 128, 4096, 3
EPS = 1e-6


def rmsnorm(x, gain):
    var = np.mean(np.square(x), axis=-1, keepdims=True)
    return x * (1.0 / np.sqrt(var + EPS)) * gain


def setup_inputs():
    s = mx_kscale(D)
    return {"x": bf(np.random.standard_normal((B, S, D))),
            "rms1_scale": bf((1.0 + 0.1 * np.random.standard_normal(D)) * s),
            "w_qkv": bf(np.random.standard_normal((D, G * H * HD)) / np.sqrt(D) / s[:, None])}


def reference(x, rms1_scale, w_qkv):
    h = rmsnorm(f64(x), f64(rms1_scale))
    qkv = mxq(h, 2, "e4m3") @ mxq(f64(w_qkv), 0, "e4m3")
    qkv = qkv.reshape(B, S, G, H, HD)
    return qkv[:, :, 0], qkv[:, :, 1], qkv[:, :, 2]

@@ -1,0 +1,206 @@
+from contextlib import ExitStack
+
+import concourse.mybir as mybir
+from concourse.masks import make_identity
+
+F32 = mybir.dt.float32
+BF16 = mybir.dt.bfloat16
+U32 = mybir.dt.uint32
+U8 = mybir.dt.uint8
+FP8X4 = mybir.dt.float8_e4m3fn_x4
+ACT = mybir.ActivationFunctionType
+ALU = mybir.AluOpType
+
+P = 128
+PACK = 4
+TOKENS = 4 * 2048
+D = 512
+PROJ = 3
+HD = 128
+N_OUT = PROJ * HD
+EPS = 1e-6
+TILES = TOKENS // P
+ROUND = 4
+ROUNDS = TILES // ROUND
+SUMS_AHEAD = 3
+
+FLOPS = 2 * TOKENS * D * N_OUT
+
+
+def tile_transformerblocktpu_pa_t_kernel(tc, x, rms1_scale, w_qkv, out_0, out_1, out_2):
+    nc = tc.nc
+    x_view = x.flatten_outer_dims().rearrange("(p t) d -> p t d", t=TILES)
+    out_views = [o.flatten_outer_dims().rearrange("(p t) d -> p t d", t=TILES) for o in (out_0, out_1, out_2)]
+
+    with ExitStack() as stack:
+        const = stack.enter_context(tc.tile_pool(name="const", bufs=1))
+        x_pool = stack.enter_context(tc.tile_pool(name="x", bufs=ROUNDS))
+        stat_pool = stack.enter_context(tc.tile_pool(name="stat", bufs=SUMS_AHEAD + 2))
+        square_pool = stack.enter_context(tc.tile_pool(name="square", bufs=ROUND))
+        scaled_pool = stack.enter_context(tc.tile_pool(name="scaled", bufs=2 * ROUND))
+        mx_pool = stack.enter_context(tc.tile_pool(name="mx", bufs=3))
+        result_pool = stack.enter_context(tc.tile_pool(name="result", bufs=9))
+        psum_t = stack.enter_context(tc.psum_pool(name="psum_t", bufs=ROUND))
+        psum_o = stack.enter_context(tc.psum_pool(name="psum_o", bufs=4))
+        stack.enter_context(tc.manual_schedule())
+
+        ident = const.tile([P, P], F32)
+        make_identity(nc, ident[:])
+
+        x_rounds = [x_pool.tile([P, ROUND, D], BF16, name="x_r") for k in range(ROUNDS)]
+
+        def load_x(k, i, n):
+            t = k * ROUND + i
+            nc.sync.dma_start(out=x_rounds[k][:, i : i + n, :], in_=x_view[:, t : t + n, :])
+
+        gain = const.tile([P, PACK], BF16)
+        w_raw = const.tile([P, PACK, N_OUT], BF16)
+        load_x(0, 0, 1)
+        load_x(0, 1, 1)
+        nc.sync.dma_start(out=w_raw[:], in_=w_qkv.rearrange("(p j) n -> p j n", j=PACK))
+        load_x(0, 2, 2)
+        nc.sync.dma_start(out=gain[:], in_=rms1_scale.rearrange("(p j) -> p j", j=PACK))
+        for k in range(1, ROUNDS):
+            load_x(k, 0, ROUND)
+
+        eps = const.tile([P, 1], F32)
+        nc.vector.memset(eps[:], EPS)
+        warm = const.tile([P, 1], F32)
+        nc.scalar.activation(out=warm[:], in_=eps[:], func=ACT.Sqrt)
+
+        w_grouped = const.tile([P, N_OUT, PACK], BF16, align_bytes=64)
+        w_codes = const.tile([P, N_OUT], U32, align_bytes=64)
+        w_scales = const.tile([P, N_OUT], U8, align_bytes=64)
+
+        def prepare_weights():
+            nc.vector.tensor_copy(out=w_grouped[:], in_=w_raw[:].rearrange("p j n -> p n j"))
+            for n0, n1 in ((0, 2 * HD), (2 * HD, 3 * HD)):
+                nc.vector.quantize_mx(
+                    out=w_codes[:, n0:n1].bitcast(FP8X4),
+                    scales=w_scales[:, n0:n1],
+                    in_=w_grouped[:, n0:n1, :].rearrange("p n j -> p (n j)"),
+                )
+
+        sums_of = {}
+        std_of = {}
+        rstd_of = {}
+        scaled_of = {}
+        turned_of = {}
+        grouped_of = {}
+        codes_of = {}
+        acc_of = {}
+
+        def x_tile(k, i):
+            return x_rounds[k][:, i, :]
+
+        def sum_squares(k):
+            sums_of[k] = stat_pool.tile([P, ROUND], F32, name="sums")
+            for i in range(ROUND):
+                squares = square_pool.tile([P, D], BF16, name="squares")
+                nc.scalar.activation(
+                    out=squares[:], in_=x_tile(k, i), func=ACT.Square, accum_out=sums_of[k][:, i : i + 1]
+                )
+
+        def root(k):
+            std_of[k] = stat_pool.tile([P, ROUND], F32, name="std")
+            nc.scalar.activation(out=std_of[k][:], in_=sums_of[k][:], func=ACT.Sqrt, scale=1.0 / D, bias=eps[:])
+
+        def invert(k):
+            rstd_of[k] = stat_pool.tile([P, ROUND], F32, name="rstd")
+            nc.vector.reciprocal(out=rstd_of[k][:], in_=std_of[k][:])
+
+        def scale(k, i, on_vector=False):
+            scaled_of[k, i] = scaled_pool.tile([P, PACK, P], F32, name="scaled")
+            rstd = rstd_of[k][:, i : i + 1]
+            src = x_tile(k, i).rearrange("p (m t) -> p t m", t=PACK)
+            if on_vector:
+                nc.vector.tensor_scalar(out=scaled_of[k, i][:], in0=src, scalar1=rstd, scalar2=None, op0=ALU.mult)
+            else:
+                nc.gpsimd.tensor_scalar(
+                    out=scaled_of[k, i][:], in0=src, scalar1=rstd, scalar2=0.0, op0=ALU.mult, op1=ALU.add
+                )
+
+        def turn(k, i):
+            turned = psum_t.tile([P, PACK, P], F32, name="turned")
+            for j in range(PACK):
+                nc.tensor.transpose(turned[:, j, :], scaled_of[k, i][:, j, :], ident[:])
+            turned_of[k, i] = turned
+
+        def apply_gain(k, i):
+            if i == 0:
+                grouped_of[k] = mx_pool.tile([P, ROUND, P, PACK], BF16, name="grouped", align_bytes=64)
+            nc.vector.tensor_tensor(
+                out=grouped_of[k][:, i, :, :],
+                in0=turned_of[k, i][:].rearrange("p j r -> p r j"),
+                in1=gain[:].unsqueeze(1).to_broadcast([P, P, PACK]),
+                op=ALU.mult,
+            )
+
+        def quantise(k):
+            codes = mx_pool.tile([P, ROUND * P], U32, name="codes", align_bytes=64)
+            scales = mx_pool.tile([P, ROUND * P], U8, name="scales", align_bytes=64)
+            nc.vector.quantize_mx(
+                out=codes[:].bitcast(FP8X4),
+                scales=scales[:],
+                in_=grouped_of[k][:].rearrange("p i r j -> p (i r j)"),
+            )
+            codes_of[k] = (codes, scales)
+
+        def project(k):
+            codes, scales = codes_of[k]
+            for q in range(PROJ):
+                acc_of[k, q] = psum_o.tile([P, ROUND, HD], F32, name="acc")
+                columns = slice(q * HD, (q + 1) * HD)
+                for i in range(ROUND):
+                    tokens = slice(i * P, (i + 1) * P)
+                    nc.tensor.matmul_mx(
+                        out=acc_of[k, q][:, i, :],
+                        lhsT=codes[:, tokens].bitcast(FP8X4),
+                        lhsT_scale=scales[:, tokens],
+                        rhs=w_codes[:, columns].bitcast(FP8X4),
+                        rhs_scale=w_scales[:, columns],
+                        start=True,
+                        stop=True,
+                    )
+
+        def copy_out(k, q, on_vector):
+            result = result_pool.tile([P, ROUND, HD], F32, name="result")
+            if on_vector:
+                nc.vector.tensor_copy(out=result[:], in_=acc_of[k, q][:])
+            else:
+                nc.scalar.copy(out=result[:], in_=acc_of[k, q][:])
+            nc.sync.dma_start(out=out_views[q][:, k * ROUND : (k + 1) * ROUND, :], in_=result[:])
+
+        prepare_weights()
+        for k in range(SUMS_AHEAD):
+            sum_squares(k)
+            root(k)
+        invert(0)
+        for i in range(ROUND):
+            scale(0, i, on_vector=True)
+            turn(0, i)
+
+        for k in range(ROUNDS + 1):
+            sums_left = k + SUMS_AHEAD < ROUNDS
+            if k + 1 < ROUNDS:
+                invert(k + 1)
+                for i in range(ROUND):
+                    scale(k + 1, i)
+            if sums_left:
+                sum_squares(k + SUMS_AHEAD)
+            if k < ROUNDS:
+                for i in range(ROUND):
+                    apply_gain(k, i)
+            if k > 0:
+                project(k - 1)
+            if k + 1 < ROUNDS:
+                for i in range(ROUND):
+                    turn(k + 1, i)
+            if k > 0:
+                copy_out(k - 1, 0, on_vector=sums_left or k == ROUNDS)
+                copy_out(k - 1, 1, on_vector=False)
+                copy_out(k - 1, 2, on_vector=False)
+            if k < ROUNDS:
+                quantise(k)
+            if sums_left:
+                root(k + SUMS_AHEAD)

@@ -22,6 +22,7 @@ EPS = 1e-6
 TILES = TOKENS // P
 ROUND = 4
 ROUNDS = TILES // ROUND
+ON_GPSIMD = 2
 SUMS_AHEAD = 3
 
 FLOPS = 2 * TOKENS * D * N_OUT
@@ -184,7 +185,7 @@ def tile_transformerblocktpu_pa_t_kernel(tc, x, rms1_scale, w_qkv, out_0, out_1,
             sums_left = k + SUMS_AHEAD < ROUNDS
             if k + 1 < ROUNDS:
                 invert(k + 1)
-                for i in range(ROUND):
+                for i in range(ON_GPSIMD):
                     scale(k + 1, i)
             if sums_left:
                 sum_squares(k + SUMS_AHEAD)
@@ -194,12 +195,16 @@ def tile_transformerblocktpu_pa_t_kernel(tc, x, rms1_scale, w_qkv, out_0, out_1,
             if k > 0:
                 project(k - 1)
             if k + 1 < ROUNDS:
-                for i in range(ROUND):
+                for i in range(ON_GPSIMD):
                     turn(k + 1, i)
             if k > 0:
-                copy_out(k - 1, 0, on_vector=sums_left or k == ROUNDS)
+                copy_out(k - 1, 0, on_vector=(sums_left and k % 2 == 0) or k == ROUNDS)
                 copy_out(k - 1, 1, on_vector=False)
                 copy_out(k - 1, 2, on_vector=False)
+            if k + 1 < ROUNDS:
+                for i in range(ON_GPSIMD, ROUND):
+                    scale(k + 1, i, on_vector=True)
+                    turn(k + 1, i)
             if k < ROUNDS:
                 quantise(k)
             if sums_left:

@@ -22,7 +22,8 @@ EPS = 1e-6
 TILES = TOKENS // P
 ROUND = 4
 ROUNDS = TILES // ROUND
-ON_GPSIMD = 2
+ON_GPSIMD = 3
+VECTOR_SUMS = ((1, 2), (1, 3))
 SUMS_AHEAD = 3
 
 FLOPS = 2 * TOKENS * D * N_OUT
@@ -98,9 +99,13 @@ def tile_transformerblocktpu_pa_t_kernel(tc, x, rms1_scale, w_qkv, out_0, out_1,
             sums_of[k] = stat_pool.tile([P, ROUND], F32, name="sums")
             for i in range(ROUND):
                 squares = square_pool.tile([P, D], BF16, name="squares")
-                nc.scalar.activation(
-                    out=squares[:], in_=x_tile(k, i), func=ACT.Square, accum_out=sums_of[k][:, i : i + 1]
-                )
+                total = sums_of[k][:, i : i + 1]
+                if (k, i) in VECTOR_SUMS:
+                    nc.vector.scalar_tensor_tensor(
+                        out=squares[:], in0=x_tile(k, i), scalar=1.0, in1=x_tile(k, i), op0=ALU.mult, op1=ALU.mult, accum_out=total
+                    )
+                else:
+                    nc.scalar.activation(out=squares[:], in_=x_tile(k, i), func=ACT.Square, accum_out=total)
 
         def root(k):
             std_of[k] = stat_pool.tile([P, ROUND], F32, name="std")
@@ -198,7 +203,7 @@ def tile_transformerblocktpu_pa_t_kernel(tc, x, rms1_scale, w_qkv, out_0, out_1,
                 for i in range(ON_GPSIMD):
                     turn(k + 1, i)
             if k > 0:
-                copy_out(k - 1, 0, on_vector=(sums_left and k % 2 == 0) or k == ROUNDS)
+                copy_out(k - 1, 0, on_vector=sums_left or k == ROUNDS)
                 copy_out(k - 1, 1, on_vector=False)
                 copy_out(k - 1, 2, on_vector=False)
             if k + 1 < ROUNDS:

@@ -18,10 +18,13 @@ D = 512
 PROJ = 3
 HD = 128
 N_OUT = PROJ * HD
+N_PASS = 512
 EPS = 1e-6
 TILES = TOKENS // P
 ROUND = 4
 ROUNDS = TILES // ROUND
+HALF = ROUND // 2
+HALVES = (0, 1)
 ON_GPSIMD = 3
 VECTOR_SUMS = ((1, 2), (1, 3))
 SUMS_AHEAD = 3
@@ -41,7 +44,7 @@ def tile_transformerblocktpu_pa_t_kernel(tc, x, rms1_scale, w_qkv, out_0, out_1,
         square_pool = stack.enter_context(tc.tile_pool(name="square", bufs=ROUND))
         scaled_pool = stack.enter_context(tc.tile_pool(name="scaled", bufs=2 * ROUND))
         mx_pool = stack.enter_context(tc.tile_pool(name="mx", bufs=3))
-        result_pool = stack.enter_context(tc.tile_pool(name="result", bufs=9))
+        result_pool = stack.enter_context(tc.tile_pool(name="result", bufs=8))
         psum_t = stack.enter_context(tc.psum_pool(name="psum_t", bufs=ROUND))
         psum_o = stack.enter_context(tc.psum_pool(name="psum_o", bufs=4))
         stack.enter_context(tc.manual_schedule())
@@ -70,18 +73,18 @@ def tile_transformerblocktpu_pa_t_kernel(tc, x, rms1_scale, w_qkv, out_0, out_1,
         warm = const.tile([P, 1], F32)
         nc.scalar.activation(out=warm[:], in_=eps[:], func=ACT.Sqrt)
 
-        w_grouped = const.tile([P, N_OUT, PACK], BF16, align_bytes=64)
-        w_codes = const.tile([P, N_OUT], U32, align_bytes=64)
-        w_scales = const.tile([P, N_OUT], U8, align_bytes=64)
+        w_grouped = const.tile([P, N_PASS, PACK], BF16, align_bytes=64)
+        nc.gpsimd.memset(w_grouped[:, N_OUT:N_PASS, :], 0.0)
+        w_codes = const.tile([P, N_PASS], U32, align_bytes=64)
+        w_scales = const.tile([P, N_PASS], U8, align_bytes=64)
 
         def prepare_weights():
-            nc.vector.tensor_copy(out=w_grouped[:], in_=w_raw[:].rearrange("p j n -> p n j"))
-            for n0, n1 in ((0, 2 * HD), (2 * HD, 3 * HD)):
-                nc.vector.quantize_mx(
-                    out=w_codes[:, n0:n1].bitcast(FP8X4),
-                    scales=w_scales[:, n0:n1],
-                    in_=w_grouped[:, n0:n1, :].rearrange("p n j -> p (n j)"),
-                )
+            nc.vector.tensor_copy(out=w_grouped[:, 0:N_OUT, :], in_=w_raw[:].rearrange("p j n -> p n j"))
+            nc.vector.quantize_mx(
+                out=w_codes[:].bitcast(FP8X4),
+                scales=w_scales[:],
+                in_=w_grouped[:].rearrange("p n j -> p (n j)"),
+            )
 
         sums_of = {}
         std_of = {}
@@ -152,30 +155,34 @@ def tile_transformerblocktpu_pa_t_kernel(tc, x, rms1_scale, w_qkv, out_0, out_1,
             )
             codes_of[k] = (codes, scales)
 
-        def project(k):
-            codes, scales = codes_of[k]
-            for q in range(PROJ):
-                acc_of[k, q] = psum_o.tile([P, ROUND, HD], F32, name="acc")
-                columns = slice(q * HD, (q + 1) * HD)
-                for i in range(ROUND):
-                    tokens = slice(i * P, (i + 1) * P)
-                    nc.tensor.matmul_mx(
-                        out=acc_of[k, q][:, i, :],
-                        lhsT=codes[:, tokens].bitcast(FP8X4),
-                        lhsT_scale=scales[:, tokens],
-                        rhs=w_codes[:, columns].bitcast(FP8X4),
-                        rhs_scale=w_scales[:, columns],
-                        start=True,
-                        stop=True,
-                    )
+        def places(half):
+            return range(half * HALF, (half + 1) * HALF)
 
-        def copy_out(k, q, on_vector):
-            result = result_pool.tile([P, ROUND, HD], F32, name="result")
-            if on_vector:
-                nc.vector.tensor_copy(out=result[:], in_=acc_of[k, q][:])
-            else:
-                nc.scalar.copy(out=result[:], in_=acc_of[k, q][:])
-            nc.sync.dma_start(out=out_views[q][:, k * ROUND : (k + 1) * ROUND, :], in_=result[:])
+        def project(k, i):
+            codes, scales = codes_of[k]
+            tokens = slice(i * P, (i + 1) * P)
+            acc_of[k, i] = psum_o.tile([P, N_PASS], F32, name="acc")
+            nc.tensor.matmul_mx(
+                out=acc_of[k, i][:],
+                lhsT=codes[:, tokens].bitcast(FP8X4),
+                lhsT_scale=scales[:, tokens],
+                rhs=w_codes[:].bitcast(FP8X4),
+                rhs_scale=w_scales[:],
+                start=True,
+                stop=True,
+            )
+
+        def copy_out(k, half, vector_helps):
+            result = result_pool.tile([P, PROJ, HALF, HD], F32, name="result")
+            for n, i in enumerate(places(half)):
+                product = acc_of[k, i][:, 0:N_OUT].rearrange("p (q d) -> p q d", q=PROJ)
+                if vector_helps and i == 1:
+                    nc.vector.tensor_copy(out=result[:, :, n, :], in_=product)
+                else:
+                    nc.scalar.copy(out=result[:, :, n, :], in_=product)
+            first_tile = k * ROUND + half * HALF
+            for q in range(PROJ):
+                nc.sync.dma_start(out=out_views[q][:, first_tile : first_tile + HALF, :], in_=result[:, q, :, :])
 
         prepare_weights()
         for k in range(SUMS_AHEAD):
@@ -194,18 +201,19 @@ def tile_transformerblocktpu_pa_t_kernel(tc, x, rms1_scale, w_qkv, out_0, out_1,
                     scale(k + 1, i)
             if sums_left:
                 sum_squares(k + SUMS_AHEAD)
-            if k < ROUNDS:
-                for i in range(ROUND):
-                    apply_gain(k, i)
-            if k > 0:
-                project(k - 1)
-            if k + 1 < ROUNDS:
-                for i in range(ON_GPSIMD):
-                    turn(k + 1, i)
-            if k > 0:
-                copy_out(k - 1, 0, on_vector=sums_left or k == ROUNDS)
-                copy_out(k - 1, 1, on_vector=False)
-                copy_out(k - 1, 2, on_vector=False)
+            for half in HALVES:
+                for i in places(half):
+                    if k < ROUNDS:
+                        apply_gain(k, i)
+                for i in places(half):
+                    if k > 0:
+                        project(k - 1, i)
+                for i in places(half):
+                    if k + 1 < ROUNDS and i < ON_GPSIMD:
+                        turn(k + 1, i)
+            for half in HALVES:
+                if k > 0:
+                    copy_out(k - 1, half, vector_helps=sums_left or k == ROUNDS)
             if k + 1 < ROUNDS:
                 for i in range(ON_GPSIMD, ROUND):
                     scale(k + 1, i, on_vector=True)

@@ -25,8 +25,9 @@ ROUND = 4
 ROUNDS = TILES // ROUND
 HALF = ROUND // 2
 HALVES = (0, 1)
+RUN = 4
 ON_GPSIMD = 3
-VECTOR_SUMS = ((1, 2), (1, 3))
+VECTOR_SUMS = ((0, 1), (1, 3))
 SUMS_AHEAD = 3
 
 FLOPS = 2 * TOKENS * D * N_OUT
@@ -40,7 +41,7 @@ def tile_transformerblocktpu_pa_t_kernel(tc, x, rms1_scale, w_qkv, out_0, out_1,
     with ExitStack() as stack:
         const = stack.enter_context(tc.tile_pool(name="const", bufs=1))
         x_pool = stack.enter_context(tc.tile_pool(name="x", bufs=ROUNDS))
-        stat_pool = stack.enter_context(tc.tile_pool(name="stat", bufs=SUMS_AHEAD + 2))
+        stat_pool = stack.enter_context(tc.tile_pool(name="stat", bufs=SUMS_AHEAD + 3))
         square_pool = stack.enter_context(tc.tile_pool(name="square", bufs=ROUND))
         scaled_pool = stack.enter_context(tc.tile_pool(name="scaled", bufs=2 * ROUND))
         mx_pool = stack.enter_context(tc.tile_pool(name="mx", bufs=3))
@@ -63,7 +64,8 @@ def tile_transformerblocktpu_pa_t_kernel(tc, x, rms1_scale, w_qkv, out_0, out_1,
         load_x(0, 0, 1)
         load_x(0, 1, 1)
         nc.sync.dma_start(out=w_raw[:], in_=w_qkv.rearrange("(p j) n -> p j n", j=PACK))
-        load_x(0, 2, 2)
+        load_x(0, 2, 1)
+        load_x(0, 3, 1)
         nc.sync.dma_start(out=gain[:], in_=rms1_scale.rearrange("(p j) -> p j", j=PACK))
         for k in range(1, ROUNDS):
             load_x(k, 0, ROUND)
@@ -78,8 +80,10 @@ def tile_transformerblocktpu_pa_t_kernel(tc, x, rms1_scale, w_qkv, out_0, out_1,
         w_codes = const.tile([P, N_PASS], U32, align_bytes=64)
         w_scales = const.tile([P, N_PASS], U8, align_bytes=64)
 
-        def prepare_weights():
+        def group_weights():
             nc.vector.tensor_copy(out=w_grouped[:, 0:N_OUT, :], in_=w_raw[:].rearrange("p j n -> p n j"))
+
+        def quantise_weights():
             nc.vector.quantize_mx(
                 out=w_codes[:].bitcast(FP8X4),
                 scales=w_scales[:],
@@ -118,12 +122,14 @@ def tile_transformerblocktpu_pa_t_kernel(tc, x, rms1_scale, w_qkv, out_0, out_1,
             rstd_of[k] = stat_pool.tile([P, ROUND], F32, name="rstd")
             nc.vector.reciprocal(out=rstd_of[k][:], in_=std_of[k][:])
 
-        def scale(k, i, on_vector=False):
+        def scale(k, i, engine):
             scaled_of[k, i] = scaled_pool.tile([P, PACK, P], F32, name="scaled")
             rstd = rstd_of[k][:, i : i + 1]
             src = x_tile(k, i).rearrange("p (m t) -> p t m", t=PACK)
-            if on_vector:
+            if engine == "vector":
                 nc.vector.tensor_scalar(out=scaled_of[k, i][:], in0=src, scalar1=rstd, scalar2=None, op0=ALU.mult)
+            elif engine == "scalar":
+                nc.scalar.activation(out=scaled_of[k, i][:], in_=src, func=ACT.Copy, scale=rstd)
             else:
                 nc.gpsimd.tensor_scalar(
                     out=scaled_of[k, i][:], in0=src, scalar1=rstd, scalar2=0.0, op0=ALU.mult, op1=ALU.add
@@ -139,21 +145,24 @@ def tile_transformerblocktpu_pa_t_kernel(tc, x, rms1_scale, w_qkv, out_0, out_1,
             if i == 0:
                 grouped_of[k] = mx_pool.tile([P, ROUND, P, PACK], BF16, name="grouped", align_bytes=64)
             nc.vector.tensor_tensor(
-                out=grouped_of[k][:, i, :, :],
-                in0=turned_of[k, i][:].rearrange("p j r -> p r j"),
-                in1=gain[:].unsqueeze(1).to_broadcast([P, P, PACK]),
+                out=grouped_of[k][:, i, :, :].rearrange("p (c n) j -> p c j n", n=RUN),
+                in0=turned_of[k, i][:].rearrange("p j (c n) -> p c j n", n=RUN),
+                in1=gain[:].unsqueeze(1).unsqueeze(3).to_broadcast([P, P // RUN, PACK, RUN]),
                 op=ALU.mult,
             )
 
-        def quantise(k):
-            codes = mx_pool.tile([P, ROUND * P], U32, name="codes", align_bytes=64)
-            scales = mx_pool.tile([P, ROUND * P], U8, name="scales", align_bytes=64)
+        def quantise(k, first, n):
+            if first == 0:
+                codes = mx_pool.tile([P, ROUND * P], U32, name="codes", align_bytes=64)
+                scales = mx_pool.tile([P, ROUND * P], U8, name="scales", align_bytes=64)
+                codes_of[k] = (codes, scales)
+            codes, scales = codes_of[k]
+            columns = slice(first * P, (first + n) * P)
             nc.vector.quantize_mx(
-                out=codes[:].bitcast(FP8X4),
-                scales=scales[:],
-                in_=grouped_of[k][:].rearrange("p i r j -> p (i r j)"),
+                out=codes[:, columns].bitcast(FP8X4),
+                scales=scales[:, columns],
+                in_=grouped_of[k][:, first : first + n, :, :].rearrange("p i r j -> p (i r j)"),
             )
-            codes_of[k] = (codes, scales)
 
         def places(half):
             return range(half * HALF, (half + 1) * HALF)
@@ -172,11 +181,11 @@ def tile_transformerblocktpu_pa_t_kernel(tc, x, rms1_scale, w_qkv, out_0, out_1,
                 stop=True,
             )
 
-        def copy_out(k, half, vector_helps):
+        def copy_out(k, half, vector_place):
             result = result_pool.tile([P, PROJ, HALF, HD], F32, name="result")
             for n, i in enumerate(places(half)):
                 product = acc_of[k, i][:, 0:N_OUT].rearrange("p (q d) -> p q d", q=PROJ)
-                if vector_helps and i == 1:
+                if i == vector_place:
                     nc.vector.tensor_copy(out=result[:, :, n, :], in_=product)
                 else:
                     nc.scalar.copy(out=result[:, :, n, :], in_=product)
@@ -184,41 +193,54 @@ def tile_transformerblocktpu_pa_t_kernel(tc, x, rms1_scale, w_qkv, out_0, out_1,
             for q in range(PROJ):
                 nc.sync.dma_start(out=out_views[q][:, first_tile : first_tile + HALF, :], in_=result[:, q, :, :])
 
-        prepare_weights()
-        for k in range(SUMS_AHEAD):
+        sum_squares(0)
+        root(0)
+        group_weights()
+        for k in range(1, SUMS_AHEAD):
             sum_squares(k)
             root(k)
         invert(0)
         for i in range(ROUND):
-            scale(0, i, on_vector=True)
+            scale(0, i, "vector")
             turn(0, i)
 
         for k in range(ROUNDS + 1):
             sums_left = k + SUMS_AHEAD < ROUNDS
-            if k + 1 < ROUNDS:
+            more = k + 1 < ROUNDS
+            if more and k > 0:
                 invert(k + 1)
                 for i in range(ON_GPSIMD):
-                    scale(k + 1, i)
+                    scale(k + 1, i, "gpsimd")
             if sums_left:
                 sum_squares(k + SUMS_AHEAD)
             for half in HALVES:
                 for i in places(half):
                     if k < ROUNDS:
                         apply_gain(k, i)
+                    if k == 0 and i == 0:
+                        invert(1)
+                        for n in range(ON_GPSIMD):
+                            scale(1, n, "gpsimd")
+                if k == ROUNDS - 1:
+                    quantise(k, half * HALF, HALF)
                 for i in places(half):
                     if k > 0:
                         project(k - 1, i)
                 for i in places(half):
-                    if k + 1 < ROUNDS and i < ON_GPSIMD:
+                    if more and i < ON_GPSIMD:
                         turn(k + 1, i)
+            if k == 0:
+                quantise_weights()
+            if more and not sums_left:
+                scale(k + 1, ROUND - 1, "scalar")
+                turn(k + 1, ROUND - 1)
             for half in HALVES:
                 if k > 0:
-                    copy_out(k - 1, half, vector_helps=sums_left or k == ROUNDS)
-            if k + 1 < ROUNDS:
-                for i in range(ON_GPSIMD, ROUND):
-                    scale(k + 1, i, on_vector=True)
-                    turn(k + 1, i)
-            if k < ROUNDS:
-                quantise(k)
+                    copy_out(k - 1, half, vector_place=1 if sums_left or k == ROUNDS else None)
+            if more and sums_left:
+                scale(k + 1, ROUND - 1, "vector")
+                turn(k + 1, ROUND - 1)
+            if k < ROUNDS - 1:
+                quantise(k, 0, ROUND)
             if sums_left:
                 root(k + SUMS_AHEAD)

@@ -27,7 +27,7 @@ HALF = ROUND // 2
 HALVES = (0, 1)
 RUN = 4
 ON_GPSIMD = 3
-VECTOR_SUMS = ((0, 1), (1, 3))
+VECTOR_SUMS = ((0, 1), (0, 2), (1, 0))
 SUMS_AHEAD = 3
 
 FLOPS = 2 * TOKENS * D * N_OUT
@@ -41,11 +41,11 @@ def tile_transformerblocktpu_pa_t_kernel(tc, x, rms1_scale, w_qkv, out_0, out_1,
     with ExitStack() as stack:
         const = stack.enter_context(tc.tile_pool(name="const", bufs=1))
         x_pool = stack.enter_context(tc.tile_pool(name="x", bufs=ROUNDS))
-        stat_pool = stack.enter_context(tc.tile_pool(name="stat", bufs=SUMS_AHEAD + 3))
+        stat_pool = stack.enter_context(tc.tile_pool(name="stat", bufs=ROUNDS))
         square_pool = stack.enter_context(tc.tile_pool(name="square", bufs=ROUND))
         scaled_pool = stack.enter_context(tc.tile_pool(name="scaled", bufs=2 * ROUND))
         mx_pool = stack.enter_context(tc.tile_pool(name="mx", bufs=3))
-        result_pool = stack.enter_context(tc.tile_pool(name="result", bufs=8))
+        result_pool = stack.enter_context(tc.tile_pool(name="result", bufs=2 * ROUNDS))
         psum_t = stack.enter_context(tc.psum_pool(name="psum_t", bufs=ROUND))
         psum_o = stack.enter_context(tc.psum_pool(name="psum_o", bufs=4))
         stack.enter_context(tc.manual_schedule())
@@ -61,13 +61,13 @@ def tile_transformerblocktpu_pa_t_kernel(tc, x, rms1_scale, w_qkv, out_0, out_1,
 
         gain = const.tile([P, PACK], BF16)
         w_raw = const.tile([P, PACK, N_OUT], BF16)
-        load_x(0, 0, 1)
-        load_x(0, 1, 1)
-        nc.sync.dma_start(out=w_raw[:], in_=w_qkv.rearrange("(p j) n -> p j n", j=PACK))
-        load_x(0, 2, 1)
-        load_x(0, 3, 1)
+        for i in range(ROUND):
+            load_x(0, i, 1)
         nc.sync.dma_start(out=gain[:], in_=rms1_scale.rearrange("(p j) -> p j", j=PACK))
-        for k in range(1, ROUNDS):
+        for half in HALVES:
+            load_x(1, half * HALF, HALF)
+        nc.sync.dma_start(out=w_raw[:], in_=w_qkv.rearrange("(p j) n -> p j n", j=PACK))
+        for k in range(2, ROUNDS):
             load_x(k, 0, ROUND)
 
         eps = const.tile([P, 1], F32)
@@ -193,16 +193,14 @@ def tile_transformerblocktpu_pa_t_kernel(tc, x, rms1_scale, w_qkv, out_0, out_1,
             for q in range(PROJ):
                 nc.sync.dma_start(out=out_views[q][:, first_tile : first_tile + HALF, :], in_=result[:, q, :, :])
 
-        sum_squares(0)
-        root(0)
-        group_weights()
-        for k in range(1, SUMS_AHEAD):
+        for k in range(SUMS_AHEAD):
             sum_squares(k)
             root(k)
         invert(0)
         for i in range(ROUND):
             scale(0, i, "vector")
             turn(0, i)
+        group_weights()
 
         for k in range(ROUNDS + 1):
             sums_left = k + SUMS_AHEAD < ROUNDS
@@ -217,12 +215,12 @@ def tile_transformerblocktpu_pa_t_kernel(tc, x, rms1_scale, w_qkv, out_0, out_1,
                 for i in places(half):
                     if k < ROUNDS:
                         apply_gain(k, i)
-                    if k == 0 and i == 0:
+                    if k == ROUNDS - 1:
+                        quantise(k, i, 1)
+                    if k == 0 and i == 1:
                         invert(1)
                         for n in range(ON_GPSIMD):
                             scale(1, n, "gpsimd")
-                if k == ROUNDS - 1:
-                    quantise(k, half * HALF, HALF)
                 for i in places(half):
                     if k > 0:
                         project(k - 1, i)
@@ -231,13 +229,14 @@ def tile_transformerblocktpu_pa_t_kernel(tc, x, rms1_scale, w_qkv, out_0, out_1,
                         turn(k + 1, i)
             if k == 0:
                 quantise_weights()
-            if more and not sums_left:
+            last_on_scalar = more and not sums_left
+            if last_on_scalar:
                 scale(k + 1, ROUND - 1, "scalar")
                 turn(k + 1, ROUND - 1)
             for half in HALVES:
                 if k > 0:
-                    copy_out(k - 1, half, vector_place=1 if sums_left or k == ROUNDS else None)
-            if more and sums_left:
+                    copy_out(k - 1, half, vector_place=1 if sums_left else 2 if k == ROUNDS else None)
+            if more and not last_on_scalar:
                 scale(k + 1, ROUND - 1, "vector")
                 turn(k + 1, ROUND - 1)
             if k < ROUNDS - 1:

@@ -12,6 +12,7 @@ ACT = mybir.ActivationFunctionType
 ALU = mybir.AluOpType
 
 P = 128
+LANES = 8
 PACK = 4
 TOKENS = 4 * 2048
 D = 512
@@ -59,15 +60,24 @@ def tile_transformerblocktpu_pa_t_kernel(tc, x, rms1_scale, w_qkv, out_0, out_1,
             t = k * ROUND + i
             nc.sync.dma_start(out=x_rounds[k][:, i : i + n, :], in_=x_view[:, t : t + n, :])
 
-        gain = const.tile([P, PACK], BF16)
+        gain_rows = const.tile([P, P], BF16)
+        nc.gpsimd.memset(gain_rows[:], 0.0)
+        gain_rows_f32 = const.tile([P, P], F32)
+        gain = const.tile([P, PACK], F32)
         w_raw = const.tile([P, PACK, N_OUT], BF16)
         for i in range(ROUND):
             load_x(0, i, 1)
-        nc.sync.dma_start(out=gain[:], in_=rms1_scale.rearrange("(p j) -> p j", j=PACK))
+        nc.sync.dma_start(
+            out=gain_rows[0:PACK, :].rearrange("t (b i) -> t b i", i=LANES),
+            in_=rms1_scale.rearrange("(b t i) -> t b i", t=PACK, i=LANES),
+        )
         for half in HALVES:
             load_x(1, half * HALF, HALF)
-        nc.sync.dma_start(out=w_raw[:], in_=w_qkv.rearrange("(p j) n -> p j n", j=PACK))
-        for k in range(2, ROUNDS):
+        load_x(2, 0, ROUND)
+        w_lanes = w_qkv.rearrange("(b t i) n -> i b t n", t=PACK, i=LANES)
+        for i in range(LANES):
+            nc.sync.dma_start(out=w_raw[i::LANES, :, :], in_=w_lanes[i])
+        for k in range(3, ROUNDS):
             load_x(k, 0, ROUND)
 
         eps = const.tile([P, 1], F32)
@@ -79,6 +89,12 @@ def tile_transformerblocktpu_pa_t_kernel(tc, x, rms1_scale, w_qkv, out_0, out_1,
         nc.gpsimd.memset(w_grouped[:, N_OUT:N_PASS, :], 0.0)
         w_codes = const.tile([P, N_PASS], U32, align_bytes=64)
         w_scales = const.tile([P, N_PASS], U8, align_bytes=64)
+
+        def turn_gain():
+            nc.gpsimd.tensor_copy(out=gain_rows_f32[:], in_=gain_rows[:])
+            bank = psum_o.tile([P, N_PASS], F32, name="acc")
+            nc.tensor.transpose(bank[:, 0:P], gain_rows_f32[:], ident[:])
+            return bank
 
         def group_weights():
             nc.vector.tensor_copy(out=w_grouped[:, 0:N_OUT, :], in_=w_raw[:].rearrange("p j n -> p n j"))
@@ -125,14 +141,15 @@ def tile_transformerblocktpu_pa_t_kernel(tc, x, rms1_scale, w_qkv, out_0, out_1,
         def scale(k, i, engine):
             scaled_of[k, i] = scaled_pool.tile([P, PACK, P], F32, name="scaled")
             rstd = rstd_of[k][:, i : i + 1]
-            src = x_tile(k, i).rearrange("p (m t) -> p t m", t=PACK)
+            src = x_tile(k, i).rearrange("p (b t i) -> p t b i", t=PACK, i=LANES)
+            out = scaled_of[k, i][:].rearrange("p t (b i) -> p t b i", i=LANES)
             if engine == "vector":
-                nc.vector.tensor_scalar(out=scaled_of[k, i][:], in0=src, scalar1=rstd, scalar2=None, op0=ALU.mult)
+                nc.vector.tensor_scalar(out=out, in0=src, scalar1=rstd, scalar2=None, op0=ALU.mult)
             elif engine == "scalar":
-                nc.scalar.activation(out=scaled_of[k, i][:], in_=src, func=ACT.Copy, scale=rstd)
+                nc.scalar.activation(out=out, in_=src, func=ACT.Copy, scale=rstd)
             else:
                 nc.gpsimd.tensor_scalar(
-                    out=scaled_of[k, i][:], in0=src, scalar1=rstd, scalar2=0.0, op0=ALU.mult, op1=ALU.add
+                    out=out, in0=src, scalar1=rstd, scalar2=0.0, op0=ALU.mult, op1=ALU.add
                 )
 
         def turn(k, i):
@@ -196,11 +213,12 @@ def tile_transformerblocktpu_pa_t_kernel(tc, x, rms1_scale, w_qkv, out_0, out_1,
         for k in range(SUMS_AHEAD):
             sum_squares(k)
             root(k)
+        gain_bank = turn_gain()
         invert(0)
         for i in range(ROUND):
             scale(0, i, "vector")
             turn(0, i)
-        group_weights()
+        nc.vector.tensor_copy(out=gain[:], in_=gain_bank[:, 0:PACK])
 
         for k in range(ROUNDS + 1):
             sums_left = k + SUMS_AHEAD < ROUNDS
@@ -228,6 +246,7 @@ def tile_transformerblocktpu_pa_t_kernel(tc, x, rms1_scale, w_qkv, out_0, out_1,
                     if more and i < ON_GPSIMD:
                         turn(k + 1, i)
             if k == 0:
+                group_weights()
                 quantise_weights()
             last_on_scalar = more and not sums_left
             if last_on_scalar:
@@ -235,7 +254,7 @@ def tile_transformerblocktpu_pa_t_kernel(tc, x, rms1_scale, w_qkv, out_0, out_1,
                 turn(k + 1, ROUND - 1)
             for half in HALVES:
                 if k > 0:
-                    copy_out(k - 1, half, vector_place=1 if sums_left else 2 if k == ROUNDS else None)
+                    copy_out(k - 1, half, vector_place=1 if sums_left and k % 2 == 0 else 2 if k == ROUNDS else None)
             if more and not last_on_scalar:
                 scale(k + 1, ROUND - 1, "vector")
                 turn(k + 1, ROUND - 1)

@@ -19,7 +19,6 @@ D = 512
 PROJ = 3
 HD = 128
 N_OUT = PROJ * HD
-N_PASS = 512
 EPS = 1e-6
 TILES = TOKENS // P
 ROUND = 4
@@ -46,7 +45,7 @@ def tile_transformerblocktpu_pa_t_kernel(tc, x, rms1_scale, w_qkv, out_0, out_1,
         square_pool = stack.enter_context(tc.tile_pool(name="square", bufs=ROUND))
         scaled_pool = stack.enter_context(tc.tile_pool(name="scaled", bufs=2 * ROUND))
         mx_pool = stack.enter_context(tc.tile_pool(name="mx", bufs=3))
-        result_pool = stack.enter_context(tc.tile_pool(name="result", bufs=2 * ROUNDS))
+        result_pool = stack.enter_context(tc.tile_pool(name="result", bufs=ROUNDS))
         psum_t = stack.enter_context(tc.psum_pool(name="psum_t", bufs=ROUND))
         psum_o = stack.enter_context(tc.psum_pool(name="psum_o", bufs=4))
         stack.enter_context(tc.manual_schedule())
@@ -85,26 +84,26 @@ def tile_transformerblocktpu_pa_t_kernel(tc, x, rms1_scale, w_qkv, out_0, out_1,
         warm = const.tile([P, 1], F32)
         nc.scalar.activation(out=warm[:], in_=eps[:], func=ACT.Sqrt)
 
-        w_grouped = const.tile([P, N_PASS, PACK], BF16, align_bytes=64)
-        nc.gpsimd.memset(w_grouped[:, N_OUT:N_PASS, :], 0.0)
-        w_codes = const.tile([P, N_PASS], U32, align_bytes=64)
-        w_scales = const.tile([P, N_PASS], U8, align_bytes=64)
+        w_grouped = const.tile([P, N_OUT, PACK], BF16, align_bytes=64)
+        w_codes = const.tile([P, N_OUT], U32, align_bytes=64)
+        w_scales = const.tile([P, N_OUT], U8, align_bytes=64)
 
         def turn_gain():
             nc.gpsimd.tensor_copy(out=gain_rows_f32[:], in_=gain_rows[:])
-            bank = psum_o.tile([P, N_PASS], F32, name="acc")
+            bank = psum_o.tile([P, ROUND * HD], F32, name="acc")
             nc.tensor.transpose(bank[:, 0:P], gain_rows_f32[:], ident[:])
             return bank
 
         def group_weights():
-            nc.vector.tensor_copy(out=w_grouped[:, 0:N_OUT, :], in_=w_raw[:].rearrange("p j n -> p n j"))
+            nc.vector.tensor_copy(out=w_grouped[:], in_=w_raw[:].rearrange("p j n -> p n j"))
 
         def quantise_weights():
-            nc.vector.quantize_mx(
-                out=w_codes[:].bitcast(FP8X4),
-                scales=w_scales[:],
-                in_=w_grouped[:].rearrange("p n j -> p (n j)"),
-            )
+            for n0, n1 in ((0, 2 * HD), (2 * HD, 3 * HD)):
+                nc.vector.quantize_mx(
+                    out=w_codes[:, n0:n1].bitcast(FP8X4),
+                    scales=w_scales[:, n0:n1],
+                    in_=w_grouped[:, n0:n1, :].rearrange("p n j -> p (n j)"),
+                )
 
         sums_of = {}
         std_of = {}
@@ -114,6 +113,7 @@ def tile_transformerblocktpu_pa_t_kernel(tc, x, rms1_scale, w_qkv, out_0, out_1,
         grouped_of = {}
         codes_of = {}
         acc_of = {}
+        result_of = {}
 
         def x_tile(k, i):
             return x_rounds[k][:, i, :]
@@ -152,6 +152,11 @@ def tile_transformerblocktpu_pa_t_kernel(tc, x, rms1_scale, w_qkv, out_0, out_1,
                     out=out, in0=src, scalar1=rstd, scalar2=0.0, op0=ALU.mult, op1=ALU.add
                 )
 
+        def scaler(k, i):
+            if k + SUMS_AHEAD > ROUNDS:
+                return "gpsimd" if i < HALF else "scalar"
+            return "gpsimd" if i < ON_GPSIMD else "vector"
+
         def turn(k, i):
             turned = psum_t.tile([P, PACK, P], F32, name="turned")
             for j in range(PACK):
@@ -184,31 +189,54 @@ def tile_transformerblocktpu_pa_t_kernel(tc, x, rms1_scale, w_qkv, out_0, out_1,
         def places(half):
             return range(half * HALF, (half + 1) * HALF)
 
-        def project(k, i):
+        def multiply(k, i, q, out):
             codes, scales = codes_of[k]
             tokens = slice(i * P, (i + 1) * P)
-            acc_of[k, i] = psum_o.tile([P, N_PASS], F32, name="acc")
+            columns = slice(q * HD, (q + 1) * HD)
             nc.tensor.matmul_mx(
-                out=acc_of[k, i][:],
+                out=out,
                 lhsT=codes[:, tokens].bitcast(FP8X4),
                 lhsT_scale=scales[:, tokens],
-                rhs=w_codes[:].bitcast(FP8X4),
-                rhs_scale=w_scales[:],
+                rhs=w_codes[:, columns].bitcast(FP8X4),
+                rhs_scale=w_scales[:, columns],
                 start=True,
                 stop=True,
             )
 
-        def copy_out(k, half, vector_place):
-            result = result_pool.tile([P, PROJ, HALF, HD], F32, name="result")
-            for n, i in enumerate(places(half)):
-                product = acc_of[k, i][:, 0:N_OUT].rearrange("p (q d) -> p q d", q=PROJ)
-                if i == vector_place:
-                    nc.vector.tensor_copy(out=result[:, :, n, :], in_=product)
-                else:
-                    nc.scalar.copy(out=result[:, :, n, :], in_=product)
-            first_tile = k * ROUND + half * HALF
+        def project_round(k):
             for q in range(PROJ):
-                nc.sync.dma_start(out=out_views[q][:, first_tile : first_tile + HALF, :], in_=result[:, q, :, :])
+                acc_of[k, q] = psum_o.tile([P, ROUND, HD], F32, name="acc")
+                for i in range(ROUND):
+                    multiply(k, i, q, acc_of[k, q][:, i, :])
+
+        def project_tile(k, i):
+            acc_of[k, i] = psum_o.tile([P, ROUND, HD], F32, name="acc")
+            for q in range(PROJ):
+                multiply(k, i, q, acc_of[k, i][:, q, :])
+
+        def copy_out(out, product, on_vector):
+            if on_vector:
+                nc.vector.tensor_copy(out=out, in_=product)
+            else:
+                nc.scalar.copy(out=out, in_=product)
+
+        def store(k, q, first, n):
+            t = k * ROUND + first
+            nc.sync.dma_start(out=out_views[q][:, t : t + n, :], in_=result_of[k][:, q, first : first + n, :])
+
+        def finish_round(k, vector_helps):
+            result_of[k] = result_pool.tile([P, PROJ, ROUND, HD], F32, name="result")
+            for q in range(PROJ):
+                copy_out(result_of[k][:, q, :, :], acc_of[k, q][:], on_vector=vector_helps and q == 0)
+                store(k, q, 0, ROUND)
+
+        def finish_by_tile(k):
+            result_of[k] = result_pool.tile([P, PROJ, ROUND, HD], F32, name="result")
+            for half in HALVES:
+                for i in places(half):
+                    copy_out(result_of[k][:, :, i, :], acc_of[k, i][:, 0:PROJ, :], on_vector=i == 2)
+                for q in range(PROJ):
+                    store(k, q, half * HALF, HALF)
 
         for k in range(SUMS_AHEAD):
             sum_squares(k)
@@ -225,39 +253,40 @@ def tile_transformerblocktpu_pa_t_kernel(tc, x, rms1_scale, w_qkv, out_0, out_1,
             more = k + 1 < ROUNDS
             if more and k > 0:
                 invert(k + 1)
-                for i in range(ON_GPSIMD):
-                    scale(k + 1, i, "gpsimd")
+                for i in range(ROUND):
+                    if scaler(k + 1, i) != "vector":
+                        scale(k + 1, i, scaler(k + 1, i))
             if sums_left:
                 sum_squares(k + SUMS_AHEAD)
-            for half in HALVES:
-                for i in places(half):
-                    if k < ROUNDS:
-                        apply_gain(k, i)
-                    if k == ROUNDS - 1:
-                        quantise(k, i, 1)
-                    if k == 0 and i == 1:
-                        invert(1)
-                        for n in range(ON_GPSIMD):
-                            scale(1, n, "gpsimd")
-                for i in places(half):
-                    if k > 0:
-                        project(k - 1, i)
-                for i in places(half):
-                    if more and i < ON_GPSIMD:
+            for i in range(ROUND):
+                if k < ROUNDS:
+                    apply_gain(k, i)
+                if k == ROUNDS - 1:
+                    quantise(k, i, 1)
+                if k == 0 and i == 1:
+                    invert(1)
+                    for n in range(ON_GPSIMD):
+                        scale(1, n, "gpsimd")
+            if k == ROUNDS:
+                for i in range(ROUND):
+                    project_tile(k - 1, i)
+                finish_by_tile(k - 1)
+            elif k > 0:
+                project_round(k - 1)
+            if more:
+                for i in range(ROUND):
+                    if scaler(k + 1, i) != "vector":
                         turn(k + 1, i)
             if k == 0:
                 group_weights()
                 quantise_weights()
-            last_on_scalar = more and not sums_left
-            if last_on_scalar:
-                scale(k + 1, ROUND - 1, "scalar")
-                turn(k + 1, ROUND - 1)
-            for half in HALVES:
-                if k > 0:
-                    copy_out(k - 1, half, vector_place=1 if sums_left and k % 2 == 0 else 2 if k == ROUNDS else None)
-            if more and not last_on_scalar:
-                scale(k + 1, ROUND - 1, "vector")
-                turn(k + 1, ROUND - 1)
+            if 0 < k < ROUNDS:
+                finish_round(k - 1, vector_helps=sums_left and k % 2 == 0)
+            if more:
+                for i in range(ROUND):
+                    if scaler(k + 1, i) == "vector":
+                        scale(k + 1, i, "vector")
+                        turn(k + 1, i)
             if k < ROUNDS - 1:
                 quantise(k, 0, ROUND)
             if sums_left:

@@ -25,9 +25,10 @@ ROUND = 4
 ROUNDS = TILES // ROUND
 HALF = ROUND // 2
 HALVES = (0, 1)
+LAST = ROUND - 1
 RUN = 4
 ON_GPSIMD = 3
-VECTOR_SUMS = ((0, 1), (0, 2), (1, 0))
+VECTOR_SUMS = ((0, 1), (0, 2), (1, 0), (1, 3))
 SUMS_AHEAD = 3
 
 FLOPS = 2 * TOKENS * D * N_OUT
@@ -118,9 +119,10 @@ def tile_transformerblocktpu_pa_t_kernel(tc, x, rms1_scale, w_qkv, out_0, out_1,
         def x_tile(k, i):
             return x_rounds[k][:, i, :]
 
-        def sum_squares(k):
-            sums_of[k] = stat_pool.tile([P, ROUND], F32, name="sums")
-            for i in range(ROUND):
+        def sum_squares(k, tiles):
+            if k not in sums_of:
+                sums_of[k] = stat_pool.tile([P, ROUND], F32, name="sums")
+            for i in tiles:
                 squares = square_pool.tile([P, D], BF16, name="squares")
                 total = sums_of[k][:, i : i + 1]
                 if (k, i) in VECTOR_SUMS:
@@ -238,15 +240,20 @@ def tile_transformerblocktpu_pa_t_kernel(tc, x, rms1_scale, w_qkv, out_0, out_1,
                 for q in range(PROJ):
                     store(k, q, half * HALF, HALF)
 
-        for k in range(SUMS_AHEAD):
-            sum_squares(k)
-            root(k)
+        sum_squares(0, range(ROUND))
+        root(0)
+        sum_squares(1, range(LAST))
         gain_bank = turn_gain()
         invert(0)
         for i in range(ROUND):
-            scale(0, i, "vector")
+            scale(0, i, "vector" if i < HALF else "gpsimd")
             turn(0, i)
         nc.vector.tensor_copy(out=gain[:], in_=gain_bank[:, 0:PACK])
+        sum_squares(1, (LAST,))
+        sum_squares(2, places(0))
+        root(1)
+        sum_squares(2, places(1))
+        root(2)
 
         for k in range(ROUNDS + 1):
             sums_left = k + SUMS_AHEAD < ROUNDS
@@ -257,16 +264,18 @@ def tile_transformerblocktpu_pa_t_kernel(tc, x, rms1_scale, w_qkv, out_0, out_1,
                     if scaler(k + 1, i) != "vector":
                         scale(k + 1, i, scaler(k + 1, i))
             if sums_left:
-                sum_squares(k + SUMS_AHEAD)
+                sum_squares(k + SUMS_AHEAD, range(ROUND))
             for i in range(ROUND):
                 if k < ROUNDS:
                     apply_gain(k, i)
-                if k == ROUNDS - 1:
-                    quantise(k, i, 1)
+                if k == ROUNDS - 1 and i > 0:
+                    quantise(k, i - 1, 1)
                 if k == 0 and i == 1:
                     invert(1)
                     for n in range(ON_GPSIMD):
                         scale(1, n, "gpsimd")
+            if k == ROUNDS - 1:
+                quantise(k, ROUND - 1, 1)
             if k == ROUNDS:
                 for i in range(ROUND):
                     project_tile(k - 1, i)
@@ -279,15 +288,19 @@ def tile_transformerblocktpu_pa_t_kernel(tc, x, rms1_scale, w_qkv, out_0, out_1,
                         turn(k + 1, i)
             if k == 0:
                 group_weights()
-                quantise_weights()
             if 0 < k < ROUNDS:
-                finish_round(k - 1, vector_helps=sums_left and k % 2 == 0)
+                finish_round(k - 1, vector_helps=sums_left and k % 3 != 0)
             if more:
                 for i in range(ROUND):
                     if scaler(k + 1, i) == "vector":
                         scale(k + 1, i, "vector")
                         turn(k + 1, i)
-            if k < ROUNDS - 1:
+            if k == 0:
+                quantise_weights()
+            if k < ROUNDS - 1 and sums_left:
                 quantise(k, 0, ROUND)
+            elif k < ROUNDS - 1:
+                for half in HALVES:
+                    quantise(k, half * HALF, HALF)
             if sums_left:
                 root(k + SUMS_AHEAD)

from contextlib import ExitStack

import concourse.mybir as mybir
from concourse.masks import make_identity

F32 = mybir.dt.float32
BF16 = mybir.dt.bfloat16
U32 = mybir.dt.uint32
U8 = mybir.dt.uint8
FP8X4 = mybir.dt.float8_e4m3fn_x4
ACT = mybir.ActivationFunctionType
ALU = mybir.AluOpType

P = 128
LANES = 8
PACK = 4
TOKENS = 4 * 2048
D = 512
PROJ = 3
HD = 128
N_OUT = PROJ * HD
EPS = 1e-6
TILES = TOKENS // P
ROUND = 4
ROUNDS = TILES // ROUND
HALF = ROUND // 2
HALVES = (0, 1)
LAST = ROUND - 1
RUN = 4
ON_GPSIMD = 3
VECTOR_SUMS = ((0, 1), (0, 2), (1, 0), (1, 3))
SUMS_AHEAD = 3

FLOPS = 2 * TOKENS * D * N_OUT


def tile_transformerblocktpu_pa_t_kernel(tc, x, rms1_scale, w_qkv, out_0, out_1, out_2):
    nc = tc.nc
    x_view = x.flatten_outer_dims().rearrange("(p t) d -> p t d", t=TILES)
    out_views = [o.flatten_outer_dims().rearrange("(p t) d -> p t d", t=TILES) for o in (out_0, out_1, out_2)]

    with ExitStack() as stack:
        const = stack.enter_context(tc.tile_pool(name="const", bufs=1))
        x_pool = stack.enter_context(tc.tile_pool(name="x", bufs=ROUNDS))
        stat_pool = stack.enter_context(tc.tile_pool(name="stat", bufs=ROUNDS))
        square_pool = stack.enter_context(tc.tile_pool(name="square", bufs=ROUND))
        scaled_pool = stack.enter_context(tc.tile_pool(name="scaled", bufs=2 * ROUND))
        mx_pool = stack.enter_context(tc.tile_pool(name="mx", bufs=3))
        result_pool = stack.enter_context(tc.tile_pool(name="result", bufs=ROUNDS))
        psum_t = stack.enter_context(tc.psum_pool(name="psum_t", bufs=ROUND))
        psum_o = stack.enter_context(tc.psum_pool(name="psum_o", bufs=4))
        stack.enter_context(tc.manual_schedule())

        ident = const.tile([P, P], F32)
        make_identity(nc, ident[:])

        x_rounds = [x_pool.tile([P, ROUND, D], BF16, name="x_r") for k in range(ROUNDS)]

        def load_x(k, i, n):
            t = k * ROUND + i
            nc.sync.dma_start(out=x_rounds[k][:, i : i + n, :], in_=x_view[:, t : t + n, :])

        gain_rows = const.tile([P, P], BF16)
        nc.gpsimd.memset(gain_rows[:], 0.0)
        gain_rows_f32 = const.tile([P, P], F32)
        gain = const.tile([P, PACK], F32)
        w_raw = const.tile([P, PACK, N_OUT], BF16)
        for i in range(ROUND):
            load_x(0, i, 1)
        nc.sync.dma_start(
            out=gain_rows[0:PACK, :].rearrange("t (b i) -> t b i", i=LANES),
            in_=rms1_scale.rearrange("(b t i) -> t b i", t=PACK, i=LANES),
        )
        for half in HALVES:
            load_x(1, half * HALF, HALF)
        load_x(2, 0, ROUND)
        w_lanes = w_qkv.rearrange("(b t i) n -> i b t n", t=PACK, i=LANES)
        for i in range(LANES):
            nc.sync.dma_start(out=w_raw[i::LANES, :, :], in_=w_lanes[i])
        for k in range(3, ROUNDS):
            load_x(k, 0, ROUND)

        eps = const.tile([P, 1], F32)
        nc.vector.memset(eps[:], EPS)
        warm = const.tile([P, 1], F32)
        nc.scalar.activation(out=warm[:], in_=eps[:], func=ACT.Sqrt)

        w_grouped = const.tile([P, N_OUT, PACK], BF16, align_bytes=64)
        w_codes = const.tile([P, N_OUT], U32, align_bytes=64)
        w_scales = const.tile([P, N_OUT], U8, align_bytes=64)

        def turn_gain():
            nc.gpsimd.tensor_copy(out=gain_rows_f32[:], in_=gain_rows[:])
            bank = psum_o.tile([P, ROUND * HD], F32, name="acc")
            nc.tensor.transpose(bank[:, 0:P], gain_rows_f32[:], ident[:])
            return bank

        def group_weights():
            nc.vector.tensor_copy(out=w_grouped[:], in_=w_raw[:].rearrange("p j n -> p n j"))

        def quantise_weights():
            for n0, n1 in ((0, 2 * HD), (2 * HD, 3 * HD)):
                nc.vector.quantize_mx(
                    out=w_codes[:, n0:n1].bitcast(FP8X4),
                    scales=w_scales[:, n0:n1],
                    in_=w_grouped[:, n0:n1, :].rearrange("p n j -> p (n j)"),
                )

        sums_of = {}
        std_of = {}
        rstd_of = {}
        scaled_of = {}
        turned_of = {}
        grouped_of = {}
        codes_of = {}
        acc_of = {}
        result_of = {}

        def x_tile(k, i):
            return x_rounds[k][:, i, :]

        def sum_squares(k, tiles):
            if k not in sums_of:
                sums_of[k] = stat_pool.tile([P, ROUND], F32, name="sums")
            for i in tiles:
                squares = square_pool.tile([P, D], BF16, name="squares")
                total = sums_of[k][:, i : i + 1]
                if (k, i) in VECTOR_SUMS:
                    nc.vector.scalar_tensor_tensor(
                        out=squares[:], in0=x_tile(k, i), scalar=1.0, in1=x_tile(k, i), op0=ALU.mult, op1=ALU.mult, accum_out=total
                    )
                else:
                    nc.scalar.activation(out=squares[:], in_=x_tile(k, i), func=ACT.Square, accum_out=total)

        def root(k):
            std_of[k] = stat_pool.tile([P, ROUND], F32, name="std")
            nc.scalar.activation(out=std_of[k][:], in_=sums_of[k][:], func=ACT.Sqrt, scale=1.0 / D, bias=eps[:])

        def invert(k):
            rstd_of[k] = stat_pool.tile([P, ROUND], F32, name="rstd")
            nc.vector.reciprocal(out=rstd_of[k][:], in_=std_of[k][:])

        def scale(k, i, engine):
            scaled_of[k, i] = scaled_pool.tile([P, PACK, P], F32, name="scaled")
            rstd = rstd_of[k][:, i : i + 1]
            src = x_tile(k, i).rearrange("p (b t i) -> p t b i", t=PACK, i=LANES)
            out = scaled_of[k, i][:].rearrange("p t (b i) -> p t b i", i=LANES)
            if engine == "vector":
                nc.vector.tensor_scalar(out=out, in0=src, scalar1=rstd, scalar2=None, op0=ALU.mult)
            elif engine == "scalar":
                nc.scalar.activation(out=out, in_=src, func=ACT.Copy, scale=rstd)
            else:
                nc.gpsimd.tensor_scalar(
                    out=out, in0=src, scalar1=rstd, scalar2=0.0, op0=ALU.mult, op1=ALU.add
                )

        def scaler(k, i):
            if k + SUMS_AHEAD > ROUNDS:
                return "gpsimd" if i < HALF else "scalar"
            return "gpsimd" if i < ON_GPSIMD else "vector"

        def turn(k, i):
            turned = psum_t.tile([P, PACK, P], F32, name="turned")
            for j in range(PACK):
                nc.tensor.transpose(turned[:, j, :], scaled_of[k, i][:, j, :], ident[:])
            turned_of[k, i] = turned

        def apply_gain(k, i):
            if i == 0:
                grouped_of[k] = mx_pool.tile([P, ROUND, P, PACK], BF16, name="grouped", align_bytes=64)
            nc.vector.tensor_tensor(
                out=grouped_of[k][:, i, :, :].rearrange("p (c n) j -> p c j n", n=RUN),
                in0=turned_of[k, i][:].rearrange("p j (c n) -> p c j n", n=RUN),
                in1=gain[:].unsqueeze(1).unsqueeze(3).to_broadcast([P, P // RUN, PACK, RUN]),
                op=ALU.mult,
            )

        def quantise(k, first, n):
            if first == 0:
                codes = mx_pool.tile([P, ROUND * P], U32, name="codes", align_bytes=64)
                scales = mx_pool.tile([P, ROUND * P], U8, name="scales", align_bytes=64)
                codes_of[k] = (codes, scales)
            codes, scales = codes_of[k]
            columns = slice(first * P, (first + n) * P)
            nc.vector.quantize_mx(
                out=codes[:, columns].bitcast(FP8X4),
                scales=scales[:, columns],
                in_=grouped_of[k][:, first : first + n, :, :].rearrange("p i r j -> p (i r j)"),
            )

        def places(half):
            return range(half * HALF, (half + 1) * HALF)

        def multiply(k, i, q, out):
            codes, scales = codes_of[k]
            tokens = slice(i * P, (i + 1) * P)
            columns = slice(q * HD, (q + 1) * HD)
            nc.tensor.matmul_mx(
                out=out,
                lhsT=codes[:, tokens].bitcast(FP8X4),
                lhsT_scale=scales[:, tokens],
                rhs=w_codes[:, columns].bitcast(FP8X4),
                rhs_scale=w_scales[:, columns],
                start=True,
                stop=True,
            )

        def project_round(k):
            for q in range(PROJ):
                acc_of[k, q] = psum_o.tile([P, ROUND, HD], F32, name="acc")
                for i in range(ROUND):
                    multiply(k, i, q, acc_of[k, q][:, i, :])

        def project_tile(k, i):
            acc_of[k, i] = psum_o.tile([P, ROUND, HD], F32, name="acc")
            for q in range(PROJ):
                multiply(k, i, q, acc_of[k, i][:, q, :])

        def copy_out(out, product, on_vector):
            if on_vector:
                nc.vector.tensor_copy(out=out, in_=product)
            else:
                nc.scalar.copy(out=out, in_=product)

        def store(k, q, first, n):
            t = k * ROUND + first
            nc.sync.dma_start(out=out_views[q][:, t : t + n, :], in_=result_of[k][:, q, first : first + n, :])

        def finish_round(k, vector_helps):
            result_of[k] = result_pool.tile([P, PROJ, ROUND, HD], F32, name="result")
            for q in range(PROJ):
                copy_out(result_of[k][:, q, :, :], acc_of[k, q][:], on_vector=vector_helps and q == 0)
                store(k, q, 0, ROUND)

        def finish_by_tile(k):
            result_of[k] = result_pool.tile([P, PROJ, ROUND, HD], F32, name="result")
            for half in HALVES:
                for i in places(half):
                    copy_out(result_of[k][:, :, i, :], acc_of[k, i][:, 0:PROJ, :], on_vector=i == 2)
                for q in range(PROJ):
                    store(k, q, half * HALF, HALF)

        sum_squares(0, range(ROUND))
        root(0)
        sum_squares(1, range(LAST))
        gain_bank = turn_gain()
        invert(0)
        for i in range(ROUND):
            scale(0, i, "vector" if i < HALF else "gpsimd")
            turn(0, i)
        nc.vector.tensor_copy(out=gain[:], in_=gain_bank[:, 0:PACK])
        sum_squares(1, (LAST,))
        sum_squares(2, places(0))
        root(1)
        sum_squares(2, places(1))
        root(2)

        for k in range(ROUNDS + 1):
            sums_left = k + SUMS_AHEAD < ROUNDS
            more = k + 1 < ROUNDS
            if more and k > 0:
                invert(k + 1)
                for i in range(ROUND):
                    if scaler(k + 1, i) != "vector":
                        scale(k + 1, i, scaler(k + 1, i))
            if sums_left:
                sum_squares(k + SUMS_AHEAD, range(ROUND))
            for i in range(ROUND):
                if k < ROUNDS:
                    apply_gain(k, i)
                if k == ROUNDS - 1 and i > 0:
                    quantise(k, i - 1, 1)
                if k == 0 and i == 1:
                    invert(1)
                    for n in range(ON_GPSIMD):
                        scale(1, n, "gpsimd")
            if k == ROUNDS - 1:
                quantise(k, ROUND - 1, 1)
            if k == ROUNDS:
                for i in range(ROUND):
                    project_tile(k - 1, i)
                finish_by_tile(k - 1)
            elif k > 0:
                project_round(k - 1)
            if more:
                for i in range(ROUND):
                    if scaler(k + 1, i) != "vector":
                        turn(k + 1, i)
            if k == 0:
                group_weights()
            if 0 < k < ROUNDS:
                finish_round(k - 1, vector_helps=sums_left and k % 3 != 0)
            if more:
                for i in range(ROUND):
                    if scaler(k + 1, i) == "vector":
                        scale(k + 1, i, "vector")
                        turn(k + 1, i)
            if k == 0:
                quantise_weights()
            if k < ROUNDS - 1 and sums_left:
                quantise(k, 0, ROUND)
            elif k < ROUNDS - 1:
                for half in HALVES:
                    quantise(k, half * HALF, HALF)
            if sums_left:
                root(k + SUMS_AHEAD)
